import numpy as np
import ml_dtypes


def mxq(x, axis, fmt="e4m3"):
    dtype, down = {"e4m3": (ml_dtypes.float8_e4m3fn, 7), "e5m2": (ml_dtypes.float8_e5m2, 14)}[fmt]
    v = np.moveaxis(np.asarray(x, np.float32).astype(ml_dtypes.bfloat16).astype(np.float64), axis, -1)
    blocks = v.reshape(v.shape[:-1] + (-1, 32))
    amax = np.abs(blocks).max(-1, keepdims=True)
    byte = np.maximum(np.where(amax > 0, np.frexp(amax)[1] - 1 + 127, 0) - down, 1)
    scale = np.exp2(byte - 127.0)
    codes = (blocks / scale).astype(np.float32).astype(dtype).astype(np.float64)
    return np.moveaxis((codes * scale).reshape(v.shape), -1, axis)


WIDE = False


def mx_kscale(k):
    if not WIDE:
        return np.ones(k)
    levels = np.array([10, -10, 5, -5, 0])
    a = np.random.permutation(np.resize(levels, k // 512 * 4)).reshape(k // 512, 4)
    idx = np.arange(k)
    return np.exp2(a[idx // 512, idx % 128 // 32])


BF16 = ml_dtypes.bfloat16


def bf(x):
    return np.asarray(x, np.float32).astype(BF16)


def f64(x):
    return np.asarray(x).astype(np.float64)


N, K, D_IN, HC, H = 128, 8, 1024, 16384, 128


def sigmoid(v):
    return 1.0 / (1.0 + np.exp(-v))


def setup_inputs():
    s, t = mx_kscale(D_IN), mx_kscale(HC)
    return {
        "x": bf(np.random.standard_normal((N, D_IN)) * s),
        "child_h": bf(np.random.standard_normal((N, K, HC)) * t),
        "child_c": bf(np.random.standard_normal((N, K, H)) * 0.5),
        "Wf": bf(np.random.standard_normal((D_IN, H)) * 0.7 / np.sqrt(D_IN) / s[:, None]),
        "bWf": bf(np.random.standard_normal(H) * 0.3),
        "Uf": bf(np.random.standard_normal((HC, H)) * 0.7 / np.sqrt(HC) / t[:, None]),
        "bUf": bf(np.random.standard_normal(H) * 0.3),
    }


def reference(x, child_h, child_c, Wf, bWf, Uf, bUf):
    xf = (mxq(f64(x), 1, "e4m3") @ mxq(f64(Wf), 0, "e4m3")) + f64(bWf)
    hf = mxq(f64(child_h), 2, "e4m3") @ mxq(f64(Uf), 0, "e4m3")
    f = sigmoid(xf[:, None, :] + hf + f64(bUf))
    return (f * f64(child_c)).sum(axis=1)

@@ -1,0 +1,236 @@
+from contextlib import ExitStack
+
+import concourse.mybir as mybir
+from concourse.masks import make_identity
+
+F32 = mybir.dt.float32
+BF16 = mybir.dt.bfloat16
+U32 = mybir.dt.uint32
+U8 = mybir.dt.uint8
+FP8X4 = mybir.dt.float8_e4m3fn_x4
+ADD = mybir.AluOpType.add
+MULT = mybir.AluOpType.mult
+SIGMOID = mybir.ActivationFunctionType.Sigmoid
+
+NODES, CHILDREN, D_IN, HC, H = 128, 8, 1024, 16384, 128
+FLOPS = 2 * NODES * D_IN * H + 2 * NODES * CHILDREN * HC * H
+
+P = 128
+PACK = 4
+HALVES = 2
+K_PASS = P * PACK
+X_PASSES = D_IN // K_PASS
+
+BANK_PASSES = 2
+ROUND_PASSES = 8
+ROUND_K = ROUND_PASSES * K_PASS
+CHUNKS = HC // ROUND_K
+ROUNDS = CHUNKS * CHILDREN
+WEIGHT_DMA_PASSES = 2
+
+LOADS_AHEAD = 7
+VECTOR_EVERY = 2
+
+QUANTISE_LAG = 1
+MULTIPLY_LAG = 2
+COLLECT_LAG = 3
+GATE_LAG = 4
+
+
+def tile_childsumtreelstmcell_pa_k_kernel(tc, x, child_h, child_c, Wf, bWf, Uf, bUf, out):
+    nc = tc.nc
+    with ExitStack() as ctx:
+        constants = ctx.enter_context(tc.tile_pool(name="constants", bufs=1))
+        child_rows = ctx.enter_context(tc.tile_pool(name="child_rows", bufs=LOADS_AHEAD + 1))
+        staged = ctx.enter_context(tc.tile_pool(name="staged", bufs=3))
+        weights = ctx.enter_context(tc.tile_pool(name="weights", bufs=2))
+        gates = ctx.enter_context(tc.tile_pool(name="gates", bufs=2))
+        transposed = ctx.enter_context(tc.psum_pool(name="transposed", bufs=6))
+        products = ctx.enter_context(tc.psum_pool(name="products", bufs=2))
+        ctx.enter_context(tc.manual_schedule())
+
+        def load_weights(raw, rows, passes):
+            for first in range(0, passes, WEIGHT_DMA_PASSES):
+                last = first + WEIGHT_DMA_PASSES
+                nc.sync.dma_start(
+                    out=raw[:, first:last].rearrange("p g (u e) h -> p (g u) (e h)", e=2),
+                    in_=rows[first * K_PASS : last * K_PASS, :].rearrange("(s p e) h -> p s (e h)", p=P, e=2),
+                )
+
+        def quantise_weights(raw, passes, codes, scales):
+            grouped = weights.tile([P, passes, H, PACK], BF16, align_bytes=64, name="weights_grouped")
+            nc.vector.tensor_copy(
+                out=grouped[:].rearrange("p g (c i) t -> p g c t i", i=4),
+                in_=raw[:].rearrange("p g t (c i) -> p g c t i", i=4),
+            )
+            nc.vector.quantize_mx(
+                out=codes[:].bitcast(FP8X4),
+                scales=scales[:],
+                in_=grouped[:].rearrange("p g h t -> p (g h t)"),
+            )
+
+        def transpose_rows(rows, grouped, passes, vector_empties_last):
+            words = rows[:].bitcast(F32)
+            grouped_words = grouped[:].bitcast(F32).rearrange("p (g n u) -> p g n u", n=P, u=HALVES)
+            banks = passes // BANK_PASSES
+            for b in range(banks):
+                bank = transposed.tile([P, BANK_PASSES, HALVES, P], F32, name="bank")
+                for g in range(BANK_PASSES):
+                    for u in range(HALVES):
+                        first = ((b * BANK_PASSES + g) * HALVES + u) * P
+                        nc.tensor.transpose(bank[:, g, u, :], words[:, first : first + P], identity[:])
+                target = grouped_words[:, b * BANK_PASSES : (b + 1) * BANK_PASSES]
+                source = bank[:].rearrange("p g u n -> p g n u")
+                if vector_empties_last and b == banks - 1:
+                    nc.vector.tensor_copy(out=target, in_=source)
+                else:
+                    nc.scalar.copy(out=target, in_=source)
+
+        def multiply(acc, row_codes, row_scales, weight_codes, weight_scales, passes):
+            for g in range(passes):
+                cols = slice(g * P, (g + 1) * P)
+                nc.tensor.matmul_mx(
+                    out=acc[:],
+                    lhsT=row_codes[:, cols].bitcast(FP8X4),
+                    lhsT_scale=row_scales[:, cols],
+                    rhs=weight_codes[:, cols].bitcast(FP8X4),
+                    rhs_scale=weight_scales[:, cols],
+                    start=(g == 0),
+                    stop=(g == passes - 1),
+                )
+
+        identity = constants.tile([P, P], F32, name="identity")
+        make_identity(nc, identity[:])
+        ones = constants.tile([P, P], BF16, name="ones")
+        nc.vector.memset(ones[:], 1.0)
+        bias_rows = constants.tile([P, H], BF16, name="bias_rows")
+        nc.vector.memset(bias_rows[:], 0.0)
+        warm = constants.tile([P, 1], F32, name="warm")
+        nc.vector.memset(warm[:], 0.0)
+
+        nc.scalar.dma_start(out=bias_rows[0:1, :], in_=bWf.rearrange("(o h) -> o h", o=1))
+        nc.scalar.dma_start(out=bias_rows[1:2, :], in_=bUf.rearrange("(o h) -> o h", o=1))
+        cells = constants.tile([P, CHILDREN, H], BF16, name="cells")
+        nc.scalar.dma_start(out=cells[:], in_=child_c)
+        warmed = constants.tile([P, 1], F32, name="warmed")
+        nc.scalar.activation(out=warmed[:], in_=warm[:], func=SIGMOID)
+
+        x_rows = constants.tile([P, D_IN], BF16, name="x_rows")
+        nc.sync.dma_start(out=x_rows[:], in_=x)
+        wf_raw = constants.tile([P, X_PASSES, PACK, H], BF16, name="wf_raw")
+        load_weights(wf_raw, Wf, X_PASSES)
+
+        rows_of = {}
+        uf_raw_of = {}
+
+        def load_round(r):
+            chunk, child = divmod(r, CHILDREN)
+            rows = child_rows.tile([P, ROUND_K], BF16, name="rows")
+            nc.sync.dma_start(out=rows[:], in_=child_h[:, child, chunk * ROUND_K : (chunk + 1) * ROUND_K])
+            rows_of[r] = rows
+            if child == 0:
+                uf_raw = weights.tile([P, ROUND_PASSES, PACK, H], BF16, name="uf_raw")
+                load_weights(uf_raw, Uf[chunk * ROUND_K : (chunk + 1) * ROUND_K, :], ROUND_PASSES)
+                uf_raw_of[chunk] = uf_raw
+
+        for r in range(LOADS_AHEAD):
+            load_round(r)
+
+        x_grouped = constants.tile([P, X_PASSES * P * PACK], BF16, align_bytes=64, name="x_grouped")
+        transpose_rows(x_rows, x_grouped, X_PASSES, False)
+        bias_sum = products.tile([P, H], F32, name="acc")
+        nc.tensor.matmul(out=bias_sum[:], lhsT=ones[:], rhs=bias_rows[:], start=True, stop=True)
+
+        wf_codes = constants.tile([P, X_PASSES * H], U32, align_bytes=64, name="wf_codes")
+        wf_scales = constants.tile([P, X_PASSES * H], U8, align_bytes=64, name="wf_scales")
+        quantise_weights(wf_raw, X_PASSES, wf_codes, wf_scales)
+        x_codes = constants.tile([P, X_PASSES * P], U32, align_bytes=64, name="x_codes")
+        x_scales = constants.tile([P, X_PASSES * P], U8, align_bytes=64, name="x_scales")
+        nc.vector.quantize_mx(out=x_codes[:].bitcast(FP8X4), scales=x_scales[:], in_=x_grouped[:])
+        bias = constants.tile([P, H], F32, name="bias")
+        nc.vector.tensor_copy(out=bias[:], in_=bias_sum[:])
+
+        x_product = products.tile([P, H], F32, name="acc")
+        multiply(x_product, x_codes, x_scales, wf_codes, wf_scales, X_PASSES)
+        shared = constants.tile([P, H], F32, name="shared")
+        nc.vector.tensor_tensor(out=shared[:], in0=x_product[:], in1=bias[:], op=ADD)
+
+        sums = constants.tile([P, CHILDREN, H], F32, name="sums")
+        total = constants.tile([P, H], F32, name="total")
+        grouped_of = {}
+        codes_of = {}
+        scales_of = {}
+        uf_codes_of = {}
+        uf_scales_of = {}
+        acc_of = {}
+        gate_of = {}
+
+        def quantise_uf(chunk):
+            uf_codes = weights.tile([P, ROUND_PASSES * H], U32, align_bytes=64, name="uf_codes")
+            uf_scales = weights.tile([P, ROUND_PASSES * H], U8, align_bytes=64, name="uf_scales")
+            quantise_weights(uf_raw_of[chunk], ROUND_PASSES, uf_codes, uf_scales)
+            uf_codes_of[chunk] = uf_codes
+            uf_scales_of[chunk] = uf_scales
+
+        def transpose_round(r):
+            grouped = staged.tile([P, ROUND_PASSES * P * PACK], BF16, align_bytes=64, name="grouped")
+            transpose_rows(rows_of[r], grouped, ROUND_PASSES, r % VECTOR_EVERY == VECTOR_EVERY - 1)
+            grouped_of[r] = grouped
+
+        def quantise_round(r):
+            codes = staged.tile([P, ROUND_PASSES * P], U32, align_bytes=64, name="codes")
+            scales = staged.tile([P, ROUND_PASSES * P], U8, align_bytes=64, name="scales")
+            nc.vector.quantize_mx(out=codes[:].bitcast(FP8X4), scales=scales[:], in_=grouped_of[r][:])
+            codes_of[r] = codes
+            scales_of[r] = scales
+
+        def multiply_round(r):
+            chunk = r // CHILDREN
+            acc = products.tile([P, H], F32, name="acc")
+            multiply(acc, codes_of[r], scales_of[r], uf_codes_of[chunk], uf_scales_of[chunk], ROUND_PASSES)
+            acc_of[r] = acc
+
+        def collect_round(r):
+            chunk, child = divmod(r, CHILDREN)
+            so_far = shared[:] if chunk == 0 else sums[:, child, :]
+            nc.vector.tensor_tensor(out=sums[:, child, :], in0=acc_of[r][:], in1=so_far, op=ADD)
+
+        def open_gate(r):
+            gate = gates.tile([P, H], F32, name="gate")
+            nc.scalar.activation(out=gate[:], in_=sums[:, r % CHILDREN, :], func=SIGMOID)
+            gate_of[r] = gate
+
+        def weigh_cells(r):
+            child = r % CHILDREN
+            if child == 0:
+                nc.vector.tensor_tensor(out=total[:], in0=gate_of[r][:], in1=cells[:, child, :], op=MULT)
+            else:
+                kept = gates.tile([P, H], F32, name="kept")
+                nc.vector.tensor_tensor(out=kept[:], in0=gate_of[r][:], in1=cells[:, child, :], op=MULT)
+                nc.vector.tensor_tensor(out=total[:], in0=total[:], in1=kept[:], op=ADD)
+
+        def is_round(r):
+            return 0 <= r < ROUNDS
+
+        def closes_a_child(r):
+            return ROUNDS - CHILDREN <= r < ROUNDS
+
+        for step in range(ROUNDS + GATE_LAG):
+            if step + LOADS_AHEAD < ROUNDS:
+                load_round(step + LOADS_AHEAD)
+            if closes_a_child(step - GATE_LAG):
+                open_gate(step - GATE_LAG)
+            if is_round(step - QUANTISE_LAG):
+                quantise_round(step - QUANTISE_LAG)
+            if is_round(step - COLLECT_LAG):
+                collect_round(step - COLLECT_LAG)
+            if closes_a_child(step - GATE_LAG):
+                weigh_cells(step - GATE_LAG)
+            if is_round(step) and step % CHILDREN == 0:
+                quantise_uf(step // CHILDREN)
+            if is_round(step):
+                transpose_round(step)
+            if is_round(step - MULTIPLY_LAG):
+                multiply_round(step - MULTIPLY_LAG)
+
+        nc.sync.dma_start(out=out, in_=total[:])

@@ -52,7 +52,7 @@ def tile_childsumtreelstmcell_pa_k_kernel(tc, x, child_h, child_c, Wf, bWf, Uf, 
         def load_weights(raw, rows, passes):
             for first in range(0, passes, WEIGHT_DMA_PASSES):
                 last = first + WEIGHT_DMA_PASSES
-                nc.sync.dma_start(
+                nc.scalar.dma_start(
                     out=raw[:, first:last].rearrange("p g (u e) h -> p (g u) (e h)", e=2),
                     in_=rows[first * K_PASS : last * K_PASS, :].rearrange("(s p e) h -> p s (e h)", p=P, e=2),
                 )

from contextlib import ExitStack

import concourse.mybir as mybir
from concourse.masks import make_identity

F32 = mybir.dt.float32
BF16 = mybir.dt.bfloat16
U32 = mybir.dt.uint32
U8 = mybir.dt.uint8
FP8X4 = mybir.dt.float8_e4m3fn_x4
ADD = mybir.AluOpType.add
MULT = mybir.AluOpType.mult
SIGMOID = mybir.ActivationFunctionType.Sigmoid

NODES, CHILDREN, D_IN, HC, H = 128, 8, 1024, 16384, 128
FLOPS = 2 * NODES * D_IN * H + 2 * NODES * CHILDREN * HC * H

P = 128
PACK = 4
HALVES = 2
K_PASS = P * PACK
X_PASSES = D_IN // K_PASS

BANK_PASSES = 2
ROUND_PASSES = 8
ROUND_K = ROUND_PASSES * K_PASS
CHUNKS = HC // ROUND_K
ROUNDS = CHUNKS * CHILDREN
WEIGHT_DMA_PASSES = 2

LOADS_AHEAD = 7
VECTOR_EVERY = 2

QUANTISE_LAG = 1
MULTIPLY_LAG = 2
COLLECT_LAG = 3
GATE_LAG = 4


def tile_childsumtreelstmcell_pa_k_kernel(tc, x, child_h, child_c, Wf, bWf, Uf, bUf, out):
    nc = tc.nc
    with ExitStack() as ctx:
        constants = ctx.enter_context(tc.tile_pool(name="constants", bufs=1))
        child_rows = ctx.enter_context(tc.tile_pool(name="child_rows", bufs=LOADS_AHEAD + 1))
        staged = ctx.enter_context(tc.tile_pool(name="staged", bufs=3))
        weights = ctx.enter_context(tc.tile_pool(name="weights", bufs=2))
        gates = ctx.enter_context(tc.tile_pool(name="gates", bufs=2))
        transposed = ctx.enter_context(tc.psum_pool(name="transposed", bufs=6))
        products = ctx.enter_context(tc.psum_pool(name="products", bufs=2))
        ctx.enter_context(tc.manual_schedule())

        def load_weights(raw, rows, passes):
            for first in range(0, passes, WEIGHT_DMA_PASSES):
                last = first + WEIGHT_DMA_PASSES
                nc.scalar.dma_start(
                    out=raw[:, first:last].rearrange("p g (u e) h -> p (g u) (e h)", e=2),
                    in_=rows[first * K_PASS : last * K_PASS, :].rearrange("(s p e) h -> p s (e h)", p=P, e=2),
                )

        def quantise_weights(raw, passes, codes, scales):
            grouped = weights.tile([P, passes, H, PACK], BF16, align_bytes=64, name="weights_grouped")
            nc.vector.tensor_copy(
                out=grouped[:].rearrange("p g (c i) t -> p g c t i", i=4),
                in_=raw[:].rearrange("p g t (c i) -> p g c t i", i=4),
            )
            nc.vector.quantize_mx(
                out=codes[:].bitcast(FP8X4),
                scales=scales[:],
                in_=grouped[:].rearrange("p g h t -> p (g h t)"),
            )

        def transpose_rows(rows, grouped, passes, vector_empties_last):
            words = rows[:].bitcast(F32)
            grouped_words = grouped[:].bitcast(F32).rearrange("p (g n u) -> p g n u", n=P, u=HALVES)
            banks = passes // BANK_PASSES
            for b in range(banks):
                bank = transposed.tile([P, BANK_PASSES, HALVES, P], F32, name="bank")
                for g in range(BANK_PASSES):
                    for u in range(HALVES):
                        first = ((b * BANK_PASSES + g) * HALVES + u) * P
                        nc.tensor.transpose(bank[:, g, u, :], words[:, first : first + P], identity[:])
                target = grouped_words[:, b * BANK_PASSES : (b + 1) * BANK_PASSES]
                source = bank[:].rearrange("p g u n -> p g n u")
                if vector_empties_last and b == banks - 1:
                    nc.vector.tensor_copy(out=target, in_=source)
                else:
                    nc.scalar.copy(out=target, in_=source)

        def multiply(acc, row_codes, row_scales, weight_codes, weight_scales, passes):
            for g in range(passes):
                cols = slice(g * P, (g + 1) * P)
                nc.tensor.matmul_mx(
                    out=acc[:],
                    lhsT=row_codes[:, cols].bitcast(FP8X4),
                    lhsT_scale=row_scales[:, cols],
                    rhs=weight_codes[:, cols].bitcast(FP8X4),
                    rhs_scale=weight_scales[:, cols],
                    start=(g == 0),
                    stop=(g == passes - 1),
                )

        identity = constants.tile([P, P], F32, name="identity")
        make_identity(nc, identity[:])
        ones = constants.tile([P, P], BF16, name="ones")
        nc.vector.memset(ones[:], 1.0)
        bias_rows = constants.tile([P, H], BF16, name="bias_rows")
        nc.vector.memset(bias_rows[:], 0.0)
        warm = constants.tile([P, 1], F32, name="warm")
        nc.vector.memset(warm[:], 0.0)

        nc.scalar.dma_start(out=bias_rows[0:1, :], in_=bWf.rearrange("(o h) -> o h", o=1))
        nc.scalar.dma_start(out=bias_rows[1:2, :], in_=bUf.rearrange("(o h) -> o h", o=1))
        cells = constants.tile([P, CHILDREN, H], BF16, name="cells")
        nc.scalar.dma_start(out=cells[:], in_=child_c)
        warmed = constants.tile([P, 1], F32, name="warmed")
        nc.scalar.activation(out=warmed[:], in_=warm[:], func=SIGMOID)

        x_rows = constants.tile([P, D_IN], BF16, name="x_rows")
        nc.sync.dma_start(out=x_rows[:], in_=x)
        wf_raw = constants.tile([P, X_PASSES, PACK, H], BF16, name="wf_raw")
        load_weights(wf_raw, Wf, X_PASSES)

        rows_of = {}
        uf_raw_of = {}

        def load_round(r):
            chunk, child = divmod(r, CHILDREN)
            rows = child_rows.tile([P, ROUND_K], BF16, name="rows")
            nc.sync.dma_start(out=rows[:], in_=child_h[:, child, chunk * ROUND_K : (chunk + 1) * ROUND_K])
            rows_of[r] = rows
            if child == 0:
                uf_raw = weights.tile([P, ROUND_PASSES, PACK, H], BF16, name="uf_raw")
                load_weights(uf_raw, Uf[chunk * ROUND_K : (chunk + 1) * ROUND_K, :], ROUND_PASSES)
                uf_raw_of[chunk] = uf_raw

        for r in range(LOADS_AHEAD):
            load_round(r)

        x_grouped = constants.tile([P, X_PASSES * P * PACK], BF16, align_bytes=64, name="x_grouped")
        transpose_rows(x_rows, x_grouped, X_PASSES, False)
        bias_sum = products.tile([P, H], F32, name="acc")
        nc.tensor.matmul(out=bias_sum[:], lhsT=ones[:], rhs=bias_rows[:], start=True, stop=True)

        wf_codes = constants.tile([P, X_PASSES * H], U32, align_bytes=64, name="wf_codes")
        wf_scales = constants.tile([P, X_PASSES * H], U8, align_bytes=64, name="wf_scales")
        quantise_weights(wf_raw, X_PASSES, wf_codes, wf_scales)
        x_codes = constants.tile([P, X_PASSES * P], U32, align_bytes=64, name="x_codes")
        x_scales = constants.tile([P, X_PASSES * P], U8, align_bytes=64, name="x_scales")
        nc.vector.quantize_mx(out=x_codes[:].bitcast(FP8X4), scales=x_scales[:], in_=x_grouped[:])
        bias = constants.tile([P, H], F32, name="bias")
        nc.vector.tensor_copy(out=bias[:], in_=bias_sum[:])

        x_product = products.tile([P, H], F32, name="acc")
        multiply(x_product, x_codes, x_scales, wf_codes, wf_scales, X_PASSES)
        shared = constants.tile([P, H], F32, name="shared")
        nc.vector.tensor_tensor(out=shared[:], in0=x_product[:], in1=bias[:], op=ADD)

        sums = constants.tile([P, CHILDREN, H], F32, name="sums")
        total = constants.tile([P, H], F32, name="total")
        grouped_of = {}
        codes_of = {}
        scales_of = {}
        uf_codes_of = {}
        uf_scales_of = {}
        acc_of = {}
        gate_of = {}

        def quantise_uf(chunk):
            uf_codes = weights.tile([P, ROUND_PASSES * H], U32, align_bytes=64, name="uf_codes")
            uf_scales = weights.tile([P, ROUND_PASSES * H], U8, align_bytes=64, name="uf_scales")
            quantise_weights(uf_raw_of[chunk], ROUND_PASSES, uf_codes, uf_scales)
            uf_codes_of[chunk] = uf_codes
            uf_scales_of[chunk] = uf_scales

        def transpose_round(r):
            grouped = staged.tile([P, ROUND_PASSES * P * PACK], BF16, align_bytes=64, name="grouped")
            transpose_rows(rows_of[r], grouped, ROUND_PASSES, r % VECTOR_EVERY == VECTOR_EVERY - 1)
            grouped_of[r] = grouped

        def quantise_round(r):
            codes = staged.tile([P, ROUND_PASSES * P], U32, align_bytes=64, name="codes")
            scales = staged.tile([P, ROUND_PASSES * P], U8, align_bytes=64, name="scales")
            nc.vector.quantize_mx(out=codes[:].bitcast(FP8X4), scales=scales[:], in_=grouped_of[r][:])
            codes_of[r] = codes
            scales_of[r] = scales

        def multiply_round(r):
            chunk = r // CHILDREN
            acc = products.tile([P, H], F32, name="acc")
            multiply(acc, codes_of[r], scales_of[r], uf_codes_of[chunk], uf_scales_of[chunk], ROUND_PASSES)
            acc_of[r] = acc

        def collect_round(r):
            chunk, child = divmod(r, CHILDREN)
            so_far = shared[:] if chunk == 0 else sums[:, child, :]
            nc.vector.tensor_tensor(out=sums[:, child, :], in0=acc_of[r][:], in1=so_far, op=ADD)

        def open_gate(r):
            gate = gates.tile([P, H], F32, name="gate")
            nc.scalar.activation(out=gate[:], in_=sums[:, r % CHILDREN, :], func=SIGMOID)
            gate_of[r] = gate

        def weigh_cells(r):
            child = r % CHILDREN
            if child == 0:
                nc.vector.tensor_tensor(out=total[:], in0=gate_of[r][:], in1=cells[:, child, :], op=MULT)
            else:
                kept = gates.tile([P, H], F32, name="kept")
                nc.vector.tensor_tensor(out=kept[:], in0=gate_of[r][:], in1=cells[:, child, :], op=MULT)
                nc.vector.tensor_tensor(out=total[:], in0=total[:], in1=kept[:], op=ADD)

        def is_round(r):
            return 0 <= r < ROUNDS

        def closes_a_child(r):
            return ROUNDS - CHILDREN <= r < ROUNDS

        for step in range(ROUNDS + GATE_LAG):
            if step + LOADS_AHEAD < ROUNDS:
                load_round(step + LOADS_AHEAD)
            if closes_a_child(step - GATE_LAG):
                open_gate(step - GATE_LAG)
            if is_round(step - QUANTISE_LAG):
                quantise_round(step - QUANTISE_LAG)
            if is_round(step - COLLECT_LAG):
                collect_round(step - COLLECT_LAG)
            if closes_a_child(step - GATE_LAG):
                weigh_cells(step - GATE_LAG)
            if is_round(step) and step % CHILDREN == 0:
                quantise_uf(step // CHILDREN)
            if is_round(step):
                transpose_round(step)
            if is_round(step - MULTIPLY_LAG):
                multiply_round(step - MULTIPLY_LAG)

        nc.sync.dma_start(out=out, in_=total[:])
